import numpy as np
import ml_dtypes

BF16 = ml_dtypes.bfloat16


def bf(x):
    return np.asarray(x, np.float32).astype(BF16)


def f32(x):
    return np.asarray(x, np.float32)


def f64(x):
    return np.asarray(x).astype(np.float64)


def striped(idx):
    return np.tile(idx.reshape(-1, 16).T, (8, 1))


C, S, N, P, H, R = 768, 2048, 4096, 64, 4, 2
SCALE = 0.125
W_STD = 4.0
SCORE_STD = 8.0


def setup_inputs():
    return {"w": f32(W_STD * np.random.standard_normal((C, S))), "scores": f32(SCORE_STD * np.random.standard_normal((H, N))), "offs": striped(np.concatenate([np.random.permutation(S) for _ in range(R)]))}


def reference(w, scores, offs):
    idx = offs[:16].T.reshape(-1)
    e = np.exp(SCALE * f64(scores)).reshape(H, P, P)
    attn = (e / e.sum(axis=2, keepdims=True)).mean(axis=0)
    picked = f64(w)[:, idx].reshape(C, P, P)
    return (picked * attn[None, :, :]).sum(axis=2)

@@ -1,0 +1,75 @@
+import concourse.mybir as mybir
+
+F32 = mybir.dt.float32
+U16 = mybir.dt.uint16
+ALU = mybir.AluOpType
+FUNC = mybir.ActivationFunctionType
+AXIS = mybir.AxisListType
+
+P = 128
+CHANNELS = 768
+TABLE = 2048
+ENTRIES = 4096
+HEADS = 4
+PATCHES = 64
+SCALE = 0.125
+BLOCKS = CHANNELS // P
+PIECE = 2048
+PIECES = ENTRIES // PIECE
+PIECE_PATCHES = PIECE // PATCHES
+
+
+def tile_evl_kernel(tc, w, scores, offs, out):
+    nc = tc.nc
+    with (
+        tc.tile_pool(name="held", bufs=1) as held,
+        tc.tile_pool(name="work", bufs=2) as work,
+    ):
+        offsets = held.tile([P, ENTRIES // 16], U16, name="offsets")
+        nc.sync.dma_start(offsets[:], offs)
+
+        raw = held.tile([PATCHES, HEADS, PATCHES], F32, name="raw")
+        nc.scalar.dma_start(raw[:], scores.rearrange("h (r t) -> r h t", t=PATCHES))
+
+        tables = [held.tile([P, TABLE], F32, name=f"table{b}") for b in range(BLOCKS)]
+        nc.sync.dma_start(tables[0][:], w[0:P, :])
+
+        group = [PATCHES, HEADS, PATCHES]
+        top = held.tile([PATCHES, HEADS], F32, name="top")
+        nc.vector.reduce_max(top[:], raw[:], axis=AXIS.X)
+        shifted = held.tile(group, F32, name="shifted")
+        nc.vector.tensor_tensor(shifted[:], raw[:], top[:].unsqueeze(2).to_broadcast(group), ALU.subtract)
+        e = held.tile(group, F32, name="e")
+        nc.scalar.activation(e[:], shifted[:], FUNC.Exp, scale=SCALE)
+        norm = held.tile([PATCHES, HEADS], F32, name="norm")
+        nc.vector.reduce_sum(norm[:], e[:], axis=AXIS.X)
+        nc.vector.tensor_scalar_mul(norm[:], norm[:], float(HEADS))
+        inverse = held.tile([PATCHES, HEADS], F32, name="inverse")
+        nc.vector.reciprocal(inverse[:], norm[:])
+        share = held.tile(group, F32, name="share")
+        nc.vector.tensor_tensor(share[:], e[:], inverse[:].unsqueeze(2).to_broadcast(group), ALU.mult)
+        attn = held.tile([PATCHES, PATCHES], F32, name="attn")
+        nc.vector.tensor_reduce(attn[:], share[:].rearrange("r h t -> r t h"), axis=AXIS.X, op=ALU.add)
+
+        nc.sync.dma_start(out[0:PATCHES, :], attn[:])
+        weights = [held.tile([P, PIECE], F32, name=f"weights{k}") for k in range(PIECES)]
+        for k in range(PIECES):
+            parked = out[k * PIECE_PATCHES : (k + 1) * PIECE_PATCHES, :]
+            nc.sync.dma_start(weights[k][:], parked.rearrange("r t -> (r t)").partition_broadcast(P))
+
+        for b in range(1, BLOCKS):
+            nc.sync.dma_start(tables[b][:], w[b * P : (b + 1) * P, :])
+
+        for b in range(BLOCKS):
+            sums = work.tile([P, PATCHES], F32, name="sums")
+            for k in range(PIECES):
+                product = work.tile([P, PIECE], F32, name="product")
+                picked = tables[b][:].indirect(offsets[:, k * (PIECE // 16) : (k + 1) * (PIECE // 16)])
+                nc.vector.tensor_tensor(product[:], picked, weights[k][:], ALU.mult)
+                nc.vector.tensor_reduce(
+                    sums[:, k * PIECE_PATCHES : (k + 1) * PIECE_PATCHES],
+                    product[:].rearrange("c (r t) -> c r t", t=PATCHES),
+                    axis=AXIS.X,
+                    op=ALU.add,
+                )
+            nc.sync.dma_start(out[b * P : (b + 1) * P, :], sums[:])

@@ -23,7 +23,7 @@ def tile_evl_kernel(tc, w, scores, offs, out):
     nc = tc.nc
     with (
         tc.tile_pool(name="held", bufs=1) as held,
-        tc.tile_pool(name="work", bufs=2) as work,
+        tc.tile_pool(name="work", bufs=3) as work,
     ):
         offsets = held.tile([P, ENTRIES // 16], U16, name="offsets")
         nc.sync.dma_start(offsets[:], offs)
@@ -66,10 +66,12 @@ def tile_evl_kernel(tc, w, scores, offs, out):
                 product = work.tile([P, PIECE], F32, name="product")
                 picked = tables[b][:].indirect(offsets[:, k * (PIECE // 16) : (k + 1) * (PIECE // 16)])
                 nc.vector.tensor_tensor(product[:], picked, weights[k][:], ALU.mult)
-                nc.vector.tensor_reduce(
-                    sums[:, k * PIECE_PATCHES : (k + 1) * PIECE_PATCHES],
-                    product[:].rearrange("c (r t) -> c r t", t=PATCHES),
-                    axis=AXIS.X,
-                    op=ALU.add,
-                )
+                for r in range(PIECE_PATCHES):
+                    unused = work.tile([P, PATCHES], F32, name="unused")
+                    nc.scalar.activation(
+                        unused[:],
+                        product[:, r * PATCHES : (r + 1) * PATCHES],
+                        FUNC.Copy,
+                        accum_out=sums[:, k * PIECE_PATCHES + r : k * PIECE_PATCHES + r + 1],
+                    )
             nc.sync.dma_start(out[b * P : (b + 1) * P, :], sums[:])

@@ -1,4 +1,5 @@
 import concourse.mybir as mybir
+from concourse.masks import make_identity
 
 F32 = mybir.dt.float32
 U16 = mybir.dt.uint16
@@ -17,6 +18,7 @@ BLOCKS = CHANNELS // P
 PIECE = 2048
 PIECES = ENTRIES // PIECE
 PIECE_PATCHES = PIECE // PATCHES
+LAST_BY_VECTOR = 24
 
 
 def tile_evl_kernel(tc, w, scores, offs, out):
@@ -24,6 +26,7 @@ def tile_evl_kernel(tc, w, scores, offs, out):
     with (
         tc.tile_pool(name="held", bufs=1) as held,
         tc.tile_pool(name="work", bufs=3) as work,
+        tc.psum_pool(name="psum", bufs=2) as psum,
     ):
         offsets = held.tile([P, ENTRIES // 16], U16, name="offsets")
         nc.sync.dma_start(offsets[:], offs)
@@ -60,18 +63,35 @@ def tile_evl_kernel(tc, w, scores, offs, out):
         for b in range(1, BLOCKS):
             nc.sync.dma_start(tables[b][:], w[b * P : (b + 1) * P, :])
 
+        identity = held.tile([P, P], F32, name="identity")
+        make_identity(nc, identity[:])
+
         for b in range(BLOCKS):
-            sums = work.tile([P, PATCHES], F32, name="sums")
+            product = work.tile([P, ENTRIES], F32, name="product")
             for k in range(PIECES):
-                product = work.tile([P, PIECE], F32, name="product")
                 picked = tables[b][:].indirect(offsets[:, k * (PIECE // 16) : (k + 1) * (PIECE // 16)])
-                nc.vector.tensor_tensor(product[:], picked, weights[k][:], ALU.mult)
-                for r in range(PIECE_PATCHES):
+                nc.vector.tensor_tensor(product[:, k * PIECE : (k + 1) * PIECE], picked, weights[k][:], ALU.mult)
+
+            sums = work.tile([P, PATCHES], F32, name="sums")
+            if b % 2 == 0:
+                by_key = product[:].rearrange("c (r t) -> c t r", t=PATCHES)
+                total = psum.tile([P, PATCHES], F32, name="total")
+                for t in range(PATCHES):
+                    nc.tensor.matmul(total[:], identity[:], by_key[:, t, :], start=(t == 0), stop=(t == PATCHES - 1))
+                nc.scalar.copy(sums[:], total[:])
+            else:
+                by_vector = LAST_BY_VECTOR if b == BLOCKS - 1 else 0
+                first = PATCHES - by_vector
+                if by_vector:
+                    nc.vector.tensor_reduce(
+                        sums[:, first:PATCHES],
+                        product[:, first * PATCHES : ENTRIES].rearrange("c (r t) -> c r t", t=PATCHES),
+                        axis=AXIS.X,
+                        op=ALU.add,
+                    )
+                for r in range(first):
                     unused = work.tile([P, PATCHES], F32, name="unused")
                     nc.scalar.activation(
-                        unused[:],
-                        product[:, r * PATCHES : (r + 1) * PATCHES],
-                        FUNC.Copy,
-                        accum_out=sums[:, k * PIECE_PATCHES + r : k * PIECE_PATCHES + r + 1],
+                        unused[:], product[:, r * PATCHES : (r + 1) * PATCHES], FUNC.Copy, accum_out=sums[:, r : r + 1]
                     )
             nc.sync.dma_start(out[b * P : (b + 1) * P, :], sums[:])

@@ -1,5 +1,4 @@
 import concourse.mybir as mybir
-from concourse.masks import make_identity
 
 F32 = mybir.dt.float32
 U16 = mybir.dt.uint16
@@ -15,10 +14,12 @@ HEADS = 4
 PATCHES = 64
 SCALE = 0.125
 BLOCKS = CHANNELS // P
-PIECE = 2048
-PIECES = ENTRIES // PIECE
-PIECE_PATCHES = PIECE // PATCHES
-LAST_BY_VECTOR = 24
+WIDTHS = (2048, 2048)
+FIRST_WIDTHS = (512, 512, 1024, 2048)
+
+
+def cuts(widths):
+    return [(sum(widths[:i]), width) for i, width in enumerate(widths)]
 
 
 def tile_evl_kernel(tc, w, scores, offs, out):
@@ -26,7 +27,6 @@ def tile_evl_kernel(tc, w, scores, offs, out):
     with (
         tc.tile_pool(name="held", bufs=1) as held,
         tc.tile_pool(name="work", bufs=3) as work,
-        tc.psum_pool(name="psum", bufs=2) as psum,
     ):
         offsets = held.tile([P, ENTRIES // 16], U16, name="offsets")
         nc.sync.dma_start(offsets[:], offs)
@@ -35,63 +35,62 @@ def tile_evl_kernel(tc, w, scores, offs, out):
         nc.scalar.dma_start(raw[:], scores.rearrange("h (r t) -> r h t", t=PATCHES))
 
         tables = [held.tile([P, TABLE], F32, name=f"table{b}") for b in range(BLOCKS)]
-        nc.sync.dma_start(tables[0][:], w[0:P, :])
+        nc.scalar.dma_start(tables[0][:], w[0:P, :])
 
         group = [PATCHES, HEADS, PATCHES]
         top = held.tile([PATCHES, HEADS], F32, name="top")
         nc.vector.reduce_max(top[:], raw[:], axis=AXIS.X)
-        shifted = held.tile(group, F32, name="shifted")
-        nc.vector.tensor_tensor(shifted[:], raw[:], top[:].unsqueeze(2).to_broadcast(group), ALU.subtract)
+        shift = held.tile([PATCHES, HEADS], F32, name="shift")
+        nc.vector.tensor_scalar_mul(shift[:], top[:], -SCALE)
         e = held.tile(group, F32, name="e")
-        nc.scalar.activation(e[:], shifted[:], FUNC.Exp, scale=SCALE)
         norm = held.tile([PATCHES, HEADS], F32, name="norm")
-        nc.vector.reduce_sum(norm[:], e[:], axis=AXIS.X)
-        nc.vector.tensor_scalar_mul(norm[:], norm[:], float(HEADS))
+        for h in range(HEADS):
+            nc.scalar.activation(
+                e[:, h, :], raw[:, h, :], FUNC.Exp, bias=shift[:, h : h + 1], scale=SCALE, accum_out=norm[:, h : h + 1]
+            )
         inverse = held.tile([PATCHES, HEADS], F32, name="inverse")
         nc.vector.reciprocal(inverse[:], norm[:])
         share = held.tile(group, F32, name="share")
-        nc.vector.tensor_tensor(share[:], e[:], inverse[:].unsqueeze(2).to_broadcast(group), ALU.mult)
+        nc.vector.scalar_tensor_tensor(
+            share[:], e[:], 1.0 / HEADS, inverse[:].unsqueeze(2).to_broadcast(group), ALU.mult, ALU.mult
+        )
         attn = held.tile([PATCHES, PATCHES], F32, name="attn")
         nc.vector.tensor_reduce(attn[:], share[:].rearrange("r h t -> r t h"), axis=AXIS.X, op=ALU.add)
 
         nc.sync.dma_start(out[0:PATCHES, :], attn[:])
-        weights = [held.tile([P, PIECE], F32, name=f"weights{k}") for k in range(PIECES)]
-        for k in range(PIECES):
-            parked = out[k * PIECE_PATCHES : (k + 1) * PIECE_PATCHES, :]
-            nc.sync.dma_start(weights[k][:], parked.rearrange("r t -> (r t)").partition_broadcast(P))
+        weights = held.tile([P, ENTRIES], F32, name="weights")
+        for start, width in cuts(FIRST_WIDTHS):
+            parked = out[start // PATCHES : (start + width) // PATCHES, :]
+            nc.sync.dma_start(
+                weights[:, start : start + width], parked.rearrange("r t -> (r t)").partition_broadcast(P)
+            )
 
         for b in range(1, BLOCKS):
             nc.sync.dma_start(tables[b][:], w[b * P : (b + 1) * P, :])
 
-        identity = held.tile([P, P], F32, name="identity")
-        make_identity(nc, identity[:])
-
         for b in range(BLOCKS):
-            product = work.tile([P, ENTRIES], F32, name="product")
-            for k in range(PIECES):
-                picked = tables[b][:].indirect(offsets[:, k * (PIECE // 16) : (k + 1) * (PIECE // 16)])
-                nc.vector.tensor_tensor(product[:, k * PIECE : (k + 1) * PIECE], picked, weights[k][:], ALU.mult)
-
             sums = work.tile([P, PATCHES], F32, name="sums")
-            if b % 2 == 0:
-                by_key = product[:].rearrange("c (r t) -> c t r", t=PATCHES)
-                total = psum.tile([P, PATCHES], F32, name="total")
-                for t in range(PATCHES):
-                    nc.tensor.matmul(total[:], identity[:], by_key[:, t, :], start=(t == 0), stop=(t == PATCHES - 1))
-                nc.scalar.copy(sums[:], total[:])
-            else:
-                by_vector = LAST_BY_VECTOR if b == BLOCKS - 1 else 0
-                first = PATCHES - by_vector
-                if by_vector:
+            for start, width in cuts(FIRST_WIDTHS if b == 0 else WIDTHS):
+                product = work.tile([P, max(WIDTHS)], F32, name="product")
+                picked = tables[b][:].indirect(offsets[:, start // 16 : (start + width) // 16])
+                nc.vector.tensor_tensor(product[:, :width], picked, weights[:, start : start + width], ALU.mult)
+
+                first = start // PATCHES
+                count = width // PATCHES
+                if b == BLOCKS - 1 and start + width == ENTRIES:
                     nc.vector.tensor_reduce(
-                        sums[:, first:PATCHES],
-                        product[:, first * PATCHES : ENTRIES].rearrange("c (r t) -> c r t", t=PATCHES),
+                        sums[:, first : first + count],
+                        product[:, :width].rearrange("c (r t) -> c r t", t=PATCHES),
                         axis=AXIS.X,
                         op=ALU.add,
                     )
-                for r in range(first):
-                    unused = work.tile([P, PATCHES], F32, name="unused")
-                    nc.scalar.activation(
-                        unused[:], product[:, r * PATCHES : (r + 1) * PATCHES], FUNC.Copy, accum_out=sums[:, r : r + 1]
-                    )
+                else:
+                    for r in range(count):
+                        unused = work.tile([P, PATCHES], F32, name="unused")
+                        nc.scalar.activation(
+                            unused[:],
+                            product[:, r * PATCHES : (r + 1) * PATCHES],
+                            FUNC.Copy,
+                            accum_out=sums[:, first + r : first + r + 1],
+                        )
             nc.sync.dma_start(out[b * P : (b + 1) * P, :], sums[:])

@@ -26,16 +26,18 @@ def tile_evl_kernel(tc, w, scores, offs, out):
     nc = tc.nc
     with (
         tc.tile_pool(name="held", bufs=1) as held,
+        tc.tile_pool(name="windows", bufs=2) as windows,
         tc.tile_pool(name="work", bufs=3) as work,
     ):
+        raw = held.tile([PATCHES, HEADS, PATCHES], F32, name="raw")
+        nc.sync.dma_start(raw[:], scores.rearrange("h (r t) -> r h t", t=PATCHES))
+
         offsets = held.tile([P, ENTRIES // 16], U16, name="offsets")
         nc.sync.dma_start(offsets[:], offs)
 
-        raw = held.tile([PATCHES, HEADS, PATCHES], F32, name="raw")
-        nc.scalar.dma_start(raw[:], scores.rearrange("h (r t) -> r h t", t=PATCHES))
-
-        tables = [held.tile([P, TABLE], F32, name=f"table{b}") for b in range(BLOCKS)]
-        nc.scalar.dma_start(tables[0][:], w[0:P, :])
+        warm = held.tile([PATCHES, 1], F32, name="warm")
+        nc.gpsimd.memset(warm[:], 0.0)
+        nc.scalar.activation(warm[:], warm[:], FUNC.Exp)
 
         group = [PATCHES, HEADS, PATCHES]
         top = held.tile([PATCHES, HEADS], F32, name="top")
@@ -65,14 +67,13 @@ def tile_evl_kernel(tc, w, scores, offs, out):
                 weights[:, start : start + width], parked.rearrange("r t -> (r t)").partition_broadcast(P)
             )
 
-        for b in range(1, BLOCKS):
-            nc.sync.dma_start(tables[b][:], w[b * P : (b + 1) * P, :])
-
         for b in range(BLOCKS):
+            table = windows.tile([P, TABLE], F32, name="table")
+            nc.gpsimd.dma_start(table[:], w[b * P : (b + 1) * P, :])
             sums = work.tile([P, PATCHES], F32, name="sums")
             for start, width in cuts(FIRST_WIDTHS if b == 0 else WIDTHS):
                 product = work.tile([P, max(WIDTHS)], F32, name="product")
-                picked = tables[b][:].indirect(offsets[:, start // 16 : (start + width) // 16])
+                picked = table[:].indirect(offsets[:, start // 16 : (start + width) // 16])
                 nc.vector.tensor_tensor(product[:, :width], picked, weights[:, start : start + width], ALU.mult)
 
                 first = start // PATCHES

@@ -69,7 +69,7 @@ def tile_evl_kernel(tc, w, scores, offs, out):
 
         for b in range(BLOCKS):
             table = windows.tile([P, TABLE], F32, name="table")
-            nc.gpsimd.dma_start(table[:], w[b * P : (b + 1) * P, :])
+            nc.sync.dma_start(table[:], w[b * P : (b + 1) * P, :])
             sums = work.tile([P, PATCHES], F32, name="sums")
             for start, width in cuts(FIRST_WIDTHS if b == 0 else WIDTHS):
                 product = work.tile([P, max(WIDTHS)], F32, name="product")

@@ -36,7 +36,7 @@ def tile_evl_kernel(tc, w, scores, offs, out):
         nc.sync.dma_start(offsets[:], offs)
 
         warm = held.tile([PATCHES, 1], F32, name="warm")
-        nc.gpsimd.memset(warm[:], 0.0)
+        nc.vector.memset(warm[:], 0.0)
         nc.scalar.activation(warm[:], warm[:], FUNC.Exp)
 
         group = [PATCHES, HEADS, PATCHES]

@@ -15,7 +15,6 @@ PATCHES = 64
 SCALE = 0.125
 BLOCKS = CHANNELS // P
 WIDTHS = (2048, 2048)
-FIRST_WIDTHS = (512, 512, 1024, 2048)
 
 
 def cuts(widths):
@@ -61,7 +60,7 @@ def tile_evl_kernel(tc, w, scores, offs, out):
 
         nc.sync.dma_start(out[0:PATCHES, :], attn[:])
         weights = held.tile([P, ENTRIES], F32, name="weights")
-        for start, width in cuts(FIRST_WIDTHS):
+        for start, width in cuts(WIDTHS):
             parked = out[start // PATCHES : (start + width) // PATCHES, :]
             nc.sync.dma_start(
                 weights[:, start : start + width], parked.rearrange("r t -> (r t)").partition_broadcast(P)
@@ -71,7 +70,7 @@ def tile_evl_kernel(tc, w, scores, offs, out):
             table = windows.tile([P, TABLE], F32, name="table")
             nc.sync.dma_start(table[:], w[b * P : (b + 1) * P, :])
             sums = work.tile([P, PATCHES], F32, name="sums")
-            for start, width in cuts(FIRST_WIDTHS if b == 0 else WIDTHS):
+            for start, width in cuts(WIDTHS):
                 product = work.tile([P, max(WIDTHS)], F32, name="product")
                 picked = table[:].indirect(offsets[:, start // 16 : (start + width) // 16])
                 nc.vector.tensor_tensor(product[:, :width], picked, weights[:, start : start + width], ALU.mult)

@@ -1,4 +1,5 @@
 import concourse.mybir as mybir
+from concourse.masks import make_identity
 
 F32 = mybir.dt.float32
 U16 = mybir.dt.uint16
@@ -14,83 +15,108 @@ HEADS = 4
 PATCHES = 64
 SCALE = 0.125
 BLOCKS = CHANNELS // P
-WIDTHS = (2048, 2048)
-
-
-def cuts(widths):
-    return [(sum(widths[:i]), width) for i, width in enumerate(widths)]
+RUNS = P // HEADS
+RUN = ENTRIES // RUNS
+ROWS = RUN // PATCHES
+BANK = 512
+BANKS = ENTRIES // BANK
 
 
 def tile_evl_kernel(tc, w, scores, offs, out):
     nc = tc.nc
     with (
         tc.tile_pool(name="held", bufs=1) as held,
-        tc.tile_pool(name="windows", bufs=2) as windows,
-        tc.tile_pool(name="work", bufs=3) as work,
+        tc.tile_pool(name="work", bufs=8) as work,
+        tc.psum_pool(name="psum", bufs=4) as psum,
     ):
-        raw = held.tile([PATCHES, HEADS, PATCHES], F32, name="raw")
-        nc.sync.dma_start(raw[:], scores.rearrange("h (r t) -> r h t", t=PATCHES))
+        raw = held.tile([P, ROWS, PATCHES], F32, name="raw")
+        nc.sync.dma_start(raw[:], scores.rearrange("h (g i t) -> (h g) i t", i=ROWS, t=PATCHES))
 
         offsets = held.tile([P, ENTRIES // 16], U16, name="offsets")
         nc.sync.dma_start(offsets[:], offs)
 
-        warm = held.tile([PATCHES, 1], F32, name="warm")
+        tables = []
+        for b in range(BLOCKS):
+            table = held.tile([P, TABLE], F32, name="table%d" % b)
+            nc.sync.dma_start(table[:], w[b * P : (b + 1) * P, :])
+            tables.append(table)
+
+        warm = held.tile([P, 1], F32, name="warm")
         nc.vector.memset(warm[:], 0.0)
         nc.scalar.activation(warm[:], warm[:], FUNC.Exp)
 
-        group = [PATCHES, HEADS, PATCHES]
-        top = held.tile([PATCHES, HEADS], F32, name="top")
+        identity = held.tile([P, P], F32, name="identity")
+        make_identity(nc, identity[:])
+        pick = held.tile([P, RUNS], F32, name="pick")
+        nc.vector.tensor_reduce(pick[:], identity[:].rearrange("k (h g) -> k g h", h=HEADS), axis=AXIS.X, op=ALU.add)
+
+        group = [P, ROWS, PATCHES]
+        top = held.tile([P, ROWS], F32, name="top")
         nc.vector.reduce_max(top[:], raw[:], axis=AXIS.X)
-        shift = held.tile([PATCHES, HEADS], F32, name="shift")
+        shift = held.tile([P, ROWS], F32, name="shift")
         nc.vector.tensor_scalar_mul(shift[:], top[:], -SCALE)
         e = held.tile(group, F32, name="e")
-        norm = held.tile([PATCHES, HEADS], F32, name="norm")
-        for h in range(HEADS):
+        norm = held.tile([P, ROWS], F32, name="norm")
+        for i in range(ROWS):
             nc.scalar.activation(
-                e[:, h, :], raw[:, h, :], FUNC.Exp, bias=shift[:, h : h + 1], scale=SCALE, accum_out=norm[:, h : h + 1]
+                e[:, i, :], raw[:, i, :], FUNC.Exp, bias=shift[:, i : i + 1], scale=SCALE, accum_out=norm[:, i : i + 1]
             )
-        inverse = held.tile([PATCHES, HEADS], F32, name="inverse")
+        inverse = held.tile([P, ROWS], F32, name="inverse")
         nc.vector.reciprocal(inverse[:], norm[:])
         share = held.tile(group, F32, name="share")
         nc.vector.scalar_tensor_tensor(
             share[:], e[:], 1.0 / HEADS, inverse[:].unsqueeze(2).to_broadcast(group), ALU.mult, ALU.mult
         )
-        attn = held.tile([PATCHES, PATCHES], F32, name="attn")
-        nc.vector.tensor_reduce(attn[:], share[:].rearrange("r h t -> r t h"), axis=AXIS.X, op=ALU.add)
 
-        nc.sync.dma_start(out[0:PATCHES, :], attn[:])
         weights = held.tile([P, ENTRIES], F32, name="weights")
-        for start, width in cuts(WIDTHS):
-            parked = out[start // PATCHES : (start + width) // PATCHES, :]
-            nc.sync.dma_start(
-                weights[:, start : start + width], parked.rearrange("r t -> (r t)").partition_broadcast(P)
-            )
 
-        for b in range(BLOCKS):
-            table = windows.tile([P, TABLE], F32, name="table")
-            nc.sync.dma_start(table[:], w[b * P : (b + 1) * P, :])
-            sums = work.tile([P, PATCHES], F32, name="sums")
-            for start, width in cuts(WIDTHS):
-                product = work.tile([P, max(WIDTHS)], F32, name="product")
-                picked = table[:].indirect(offsets[:, start // 16 : (start + width) // 16])
-                nc.vector.tensor_tensor(product[:, :width], picked, weights[:, start : start + width], ALU.mult)
+        def make_weights(n):
+            bank = psum.tile([P, BANK], F32, name="bank")
+            for q in range(BANK // RUN):
+                g = n * (BANK // RUN) + q
+                nc.tensor.matmul(
+                    bank[:, q * RUN : (q + 1) * RUN],
+                    pick[:, g : g + 1].to_broadcast([P, P]),
+                    share[:].rearrange("k i t -> k (i t)"),
+                    start=True,
+                    stop=True,
+                )
+            nc.scalar.copy(weights[:, n * BANK : (n + 1) * BANK], bank[:])
 
-                first = start // PATCHES
-                count = width // PATCHES
-                if b == BLOCKS - 1 and start + width == ENTRIES:
-                    nc.vector.tensor_reduce(
-                        sums[:, first : first + count],
-                        product[:, :width].rearrange("c (r t) -> c r t", t=PATCHES),
-                        axis=AXIS.X,
-                        op=ALU.add,
+        def look_up(b, sums, product, start, width):
+            picked = tables[b][:].indirect(offsets[:, start // 16 : (start + width) // 16])
+            nc.vector.tensor_tensor(product[:, :width], picked, weights[:, start : start + width], ALU.mult)
+
+            first = start // PATCHES
+            count = width // PATCHES
+            if b == BLOCKS - 1 and start + width == ENTRIES:
+                nc.vector.tensor_reduce(
+                    sums[:, first : first + count],
+                    product[:, :width].rearrange("c (r t) -> c r t", t=PATCHES),
+                    axis=AXIS.X,
+                    op=ALU.add,
+                )
+            else:
+                for r in range(count):
+                    unused = work.tile([P, PATCHES], F32, name="unused")
+                    nc.scalar.activation(
+                        unused[:],
+                        product[:, r * PATCHES : (r + 1) * PATCHES],
+                        FUNC.Copy,
+                        accum_out=sums[:, first + r : first + r + 1],
                     )
-                else:
-                    for r in range(count):
-                        unused = work.tile([P, PATCHES], F32, name="unused")
-                        nc.scalar.activation(
-                            unused[:],
-                            product[:, r * PATCHES : (r + 1) * PATCHES],
-                            FUNC.Copy,
-                            accum_out=sums[:, first + r : first + r + 1],
-                        )
-            nc.sync.dma_start(out[b * P : (b + 1) * P, :], sums[:])
+
+        for n in range(BANKS):
+            make_weights(n)
+
+        all_sums = []
+        for b in range(BLOCKS):
+            all_sums.append(held.tile([P, PATCHES], F32, name="sums%d" % b))
+        for k in range(BANKS + BLOCKS - 1):
+            for b in reversed(range(BLOCKS)):
+                n = k - b
+                if 0 <= n < BANKS:
+                    product = work.tile([P, BANK], F32, name="product")
+                    look_up(b, all_sums[b], product, n * BANK, BANK)
+                    if n == BANKS - 1:
+                        nc.sync.dma_start(out[b * P : (b + 1) * P, :], all_sums[b][:])

@@ -20,14 +20,18 @@ RUN = ENTRIES // RUNS
 ROWS = RUN // PATCHES
 BANK = 512
 BANKS = ENTRIES // BANK
+ROUND = 2 * BANK
+ROUNDS = ENTRIES // ROUND
+ROUND_PATCHES = ROUND // PATCHES
 
 
 def tile_evl_kernel(tc, w, scores, offs, out):
     nc = tc.nc
     with (
         tc.tile_pool(name="held", bufs=1) as held,
-        tc.tile_pool(name="work", bufs=8) as work,
+        tc.tile_pool(name="work", bufs=3) as work,
         tc.psum_pool(name="psum", bufs=4) as psum,
+        tc.psum_pool(name="totals", bufs=1) as totals,
     ):
         raw = held.tile([P, ROWS, PATCHES], F32, name="raw")
         nc.sync.dma_start(raw[:], scores.rearrange("h (g i t) -> (h g) i t", i=ROWS, t=PATCHES))
@@ -69,8 +73,7 @@ def tile_evl_kernel(tc, w, scores, offs, out):
         )
 
         weights = held.tile([P, ENTRIES], F32, name="weights")
-
-        def make_weights(n):
+        for n in range(BANKS):
             bank = psum.tile([P, BANK], F32, name="bank")
             for q in range(BANK // RUN):
                 g = n * (BANK // RUN) + q
@@ -83,40 +86,50 @@ def tile_evl_kernel(tc, w, scores, offs, out):
                 )
             nc.scalar.copy(weights[:, n * BANK : (n + 1) * BANK], bank[:])
 
-        def look_up(b, sums, product, start, width):
-            picked = tables[b][:].indirect(offsets[:, start // 16 : (start + width) // 16])
-            nc.vector.tensor_tensor(product[:, :width], picked, weights[:, start : start + width], ALU.mult)
+        sums = held.tile([P, BLOCKS, PATCHES], F32, name="sums")
+        total = totals.tile([P, BLOCKS, ROUND_PATCHES], F32, name="total")
 
-            first = start // PATCHES
-            count = width // PATCHES
-            if b == BLOCKS - 1 and start + width == ENTRIES:
-                nc.vector.tensor_reduce(
-                    sums[:, first : first + count],
-                    product[:, :width].rearrange("c (r t) -> c r t", t=PATCHES),
-                    axis=AXIS.X,
-                    op=ALU.add,
-                )
-            else:
-                for r in range(count):
-                    unused = work.tile([P, PATCHES], F32, name="unused")
-                    nc.scalar.activation(
-                        unused[:],
-                        product[:, r * PATCHES : (r + 1) * PATCHES],
-                        FUNC.Copy,
-                        accum_out=sums[:, first + r : first + r + 1],
+        for m in range(ROUNDS):
+            products = work.tile([P, BLOCKS, ROUND], F32, name="products")
+            for b in range(BLOCKS):
+                if m == ROUNDS - 1 and b == BLOCKS - 1:
+                    nc.vector.tensor_copy(sums[:, :, 0:ROUND_PATCHES], total[:])
+                for at in range(0, ROUND, BANK):
+                    start = m * ROUND + at
+                    picked = tables[b][:].indirect(offsets[:, start // 16 : (start + BANK) // 16])
+                    nc.vector.tensor_tensor(
+                        products[:, b, at : at + BANK], picked, weights[:, start : start + BANK], ALU.mult
+                    )
+                    first = start // PATCHES
+                    count = BANK // PATCHES
+                    if m == 0:
+                        pass
+                    elif start + BANK == ENTRIES and b == BLOCKS - 1:
+                        nc.vector.tensor_reduce(
+                            sums[:, b, first : first + count],
+                            products[:, b, at : at + BANK].rearrange("c (r t) -> c r t", t=PATCHES),
+                            axis=AXIS.X,
+                            op=ALU.add,
+                        )
+                    else:
+                        for r in range(count):
+                            unused = work.tile([P, PATCHES], F32, name="unused")
+                            nc.scalar.activation(
+                                unused[:],
+                                products[:, b, at + r * PATCHES : at + (r + 1) * PATCHES],
+                                FUNC.Copy,
+                                accum_out=sums[:, b, first + r : first + r + 1],
+                            )
+            if m == 0:
+                by_key = products[:].rearrange("c b (r t) -> c (b r) t", t=PATCHES)
+                for t in range(PATCHES):
+                    nc.tensor.matmul(
+                        total[:].rearrange("c b r -> c (b r)"),
+                        identity[:],
+                        by_key[:, :, t],
+                        start=(t == 0),
+                        stop=(t == PATCHES - 1),
                     )
 
-        for n in range(BANKS):
-            make_weights(n)
-
-        all_sums = []
         for b in range(BLOCKS):
-            all_sums.append(held.tile([P, PATCHES], F32, name="sums%d" % b))
-        for k in range(BANKS + BLOCKS - 1):
-            for b in reversed(range(BLOCKS)):
-                n = k - b
-                if 0 <= n < BANKS:
-                    product = work.tile([P, BANK], F32, name="product")
-                    look_up(b, all_sums[b], product, n * BANK, BANK)
-                    if n == BANKS - 1:
-                        nc.sync.dma_start(out[b * P : (b + 1) * P, :], all_sums[b][:])
+            nc.sync.dma_start(out[b * P : (b + 1) * P, :], sums[:, b, :])

@@ -23,6 +23,12 @@ BANKS = ENTRIES // BANK
 ROUND = 2 * BANK
 ROUNDS = ENTRIES // ROUND
 ROUND_PATCHES = ROUND // PATCHES
+OPENING = (RUN, RUN, 2 * RUN)
+assert sum(OPENING) == BANK
+
+
+def cuts(start, widths):
+    return [(start + sum(widths[:i]), width) for i, width in enumerate(widths)]
 
 
 def tile_evl_kernel(tc, w, scores, offs, out):
@@ -73,10 +79,10 @@ def tile_evl_kernel(tc, w, scores, offs, out):
         )
 
         weights = held.tile([P, ENTRIES], F32, name="weights")
-        for n in range(BANKS):
+        for start, width in cuts(0, OPENING + (BANK,) * (BANKS - 1)):
             bank = psum.tile([P, BANK], F32, name="bank")
-            for q in range(BANK // RUN):
-                g = n * (BANK // RUN) + q
+            for q in range(width // RUN):
+                g = start // RUN + q
                 nc.tensor.matmul(
                     bank[:, q * RUN : (q + 1) * RUN],
                     pick[:, g : g + 1].to_broadcast([P, P]),
@@ -84,7 +90,7 @@ def tile_evl_kernel(tc, w, scores, offs, out):
                     start=True,
                     stop=True,
                 )
-            nc.scalar.copy(weights[:, n * BANK : (n + 1) * BANK], bank[:])
+            nc.scalar.copy(weights[:, start : start + width], bank[:, :width])
 
         sums = held.tile([P, BLOCKS, PATCHES], F32, name="sums")
         total = totals.tile([P, BLOCKS, ROUND_PATCHES], F32, name="total")
@@ -94,20 +100,21 @@ def tile_evl_kernel(tc, w, scores, offs, out):
             for b in range(BLOCKS):
                 if m == ROUNDS - 1 and b == BLOCKS - 1:
                     nc.vector.tensor_copy(sums[:, :, 0:ROUND_PATCHES], total[:])
-                for at in range(0, ROUND, BANK):
+                opening = m == 0 and b == 0
+                for at, width in cuts(0, OPENING + (BANK,) if opening else (BANK, BANK)):
                     start = m * ROUND + at
-                    picked = tables[b][:].indirect(offsets[:, start // 16 : (start + BANK) // 16])
+                    picked = tables[b][:].indirect(offsets[:, start // 16 : (start + width) // 16])
                     nc.vector.tensor_tensor(
-                        products[:, b, at : at + BANK], picked, weights[:, start : start + BANK], ALU.mult
+                        products[:, b, at : at + width], picked, weights[:, start : start + width], ALU.mult
                     )
                     first = start // PATCHES
-                    count = BANK // PATCHES
+                    count = width // PATCHES
                     if m == 0:
                         pass
-                    elif start + BANK == ENTRIES and b == BLOCKS - 1:
+                    elif start + width == ENTRIES and b == BLOCKS - 1:
                         nc.vector.tensor_reduce(
                             sums[:, b, first : first + count],
-                            products[:, b, at : at + BANK].rearrange("c (r t) -> c r t", t=PATCHES),
+                            products[:, b, at : at + width].rearrange("c (r t) -> c r t", t=PATCHES),
                             axis=AXIS.X,
                             op=ALU.add,
                         )

@@ -23,8 +23,7 @@ BANKS = ENTRIES // BANK
 ROUND = 2 * BANK
 ROUNDS = ENTRIES // ROUND
 ROUND_PATCHES = ROUND // PATCHES
-OPENING = (RUN, RUN, 2 * RUN)
-assert sum(OPENING) == BANK
+OPENING = ((RUN,) * (ROUND // RUN), (BANK,) * (ROUND // BANK)) + ((ROUND,),) * (BLOCKS - 2)
 
 
 def cuts(start, widths):
@@ -79,7 +78,7 @@ def tile_evl_kernel(tc, w, scores, offs, out):
         )
 
         weights = held.tile([P, ENTRIES], F32, name="weights")
-        for start, width in cuts(0, OPENING + (BANK,) * (BANKS - 1)):
+        for start, width in cuts(0, OPENING[0] + (BANK,) * ((ENTRIES - ROUND) // BANK)):
             bank = psum.tile([P, BANK], F32, name="bank")
             for q in range(width // RUN):
                 g = start // RUN + q
@@ -100,8 +99,7 @@ def tile_evl_kernel(tc, w, scores, offs, out):
             for b in range(BLOCKS):
                 if m == ROUNDS - 1 and b == BLOCKS - 1:
                     nc.vector.tensor_copy(sums[:, :, 0:ROUND_PATCHES], total[:])
-                opening = m == 0 and b == 0
-                for at, width in cuts(0, OPENING + (BANK,) if opening else (BANK, BANK)):
+                for at, width in cuts(0, OPENING[b] if m == 0 else (BANK,) * (ROUND // BANK)):
                     start = m * ROUND + at
                     picked = tables[b][:].indirect(offsets[:, start // 16 : (start + width) // 16])
                     nc.vector.tensor_tensor(

@@ -99,7 +99,13 @@ def tile_evl_kernel(tc, w, scores, offs, out):
             for b in range(BLOCKS):
                 if m == ROUNDS - 1 and b == BLOCKS - 1:
                     nc.vector.tensor_copy(sums[:, :, 0:ROUND_PATCHES], total[:])
-                for at, width in cuts(0, OPENING[b] if m == 0 else (BANK,) * (ROUND // BANK)):
+                if m == 0:
+                    widths = OPENING[b]
+                elif m < ROUNDS - 1:
+                    widths = (ROUND,)
+                else:
+                    widths = (BANK,) * (ROUND // BANK)
+                for at, width in cuts(0, widths):
                     start = m * ROUND + at
                     picked = tables[b][:].indirect(offsets[:, start // 16 : (start + width) // 16])
                     nc.vector.tensor_tensor(

@@ -2,6 +2,7 @@ import concourse.mybir as mybir
 from concourse.masks import make_identity
 
 F32 = mybir.dt.float32
+BF16 = mybir.dt.bfloat16
 U16 = mybir.dt.uint16
 ALU = mybir.AluOpType
 FUNC = mybir.ActivationFunctionType
@@ -124,7 +125,7 @@ def tile_evl_kernel(tc, w, scores, offs, out):
                         )
                     else:
                         for r in range(count):
-                            unused = work.tile([P, PATCHES], F32, name="unused")
+                            unused = work.tile([P, PATCHES], BF16, name="unused")
                             nc.scalar.activation(
                                 unused[:],
                                 products[:, b, at + r * PATCHES : at + (r + 1) * PATCHES],

import concourse.mybir as mybir
from concourse.masks import make_identity

F32 = mybir.dt.float32
BF16 = mybir.dt.bfloat16
U16 = mybir.dt.uint16
ALU = mybir.AluOpType
FUNC = mybir.ActivationFunctionType
AXIS = mybir.AxisListType

P = 128
CHANNELS = 768
TABLE = 2048
ENTRIES = 4096
HEADS = 4
PATCHES = 64
SCALE = 0.125
BLOCKS = CHANNELS // P
RUNS = P // HEADS
RUN = ENTRIES // RUNS
ROWS = RUN // PATCHES
BANK = 512
BANKS = ENTRIES // BANK
ROUND = 2 * BANK
ROUNDS = ENTRIES // ROUND
ROUND_PATCHES = ROUND // PATCHES
OPENING = ((RUN,) * (ROUND // RUN), (BANK,) * (ROUND // BANK)) + ((ROUND,),) * (BLOCKS - 2)


def cuts(start, widths):
    return [(start + sum(widths[:i]), width) for i, width in enumerate(widths)]


def tile_evl_kernel(tc, w, scores, offs, out):
    nc = tc.nc
    with (
        tc.tile_pool(name="held", bufs=1) as held,
        tc.tile_pool(name="work", bufs=3) as work,
        tc.psum_pool(name="psum", bufs=4) as psum,
        tc.psum_pool(name="totals", bufs=1) as totals,
    ):
        raw = held.tile([P, ROWS, PATCHES], F32, name="raw")
        nc.sync.dma_start(raw[:], scores.rearrange("h (g i t) -> (h g) i t", i=ROWS, t=PATCHES))

        offsets = held.tile([P, ENTRIES // 16], U16, name="offsets")
        nc.sync.dma_start(offsets[:], offs)

        tables = []
        for b in range(BLOCKS):
            table = held.tile([P, TABLE], F32, name="table%d" % b)
            nc.sync.dma_start(table[:], w[b * P : (b + 1) * P, :])
            tables.append(table)

        warm = held.tile([P, 1], F32, name="warm")
        nc.vector.memset(warm[:], 0.0)
        nc.scalar.activation(warm[:], warm[:], FUNC.Exp)

        identity = held.tile([P, P], F32, name="identity")
        make_identity(nc, identity[:])
        pick = held.tile([P, RUNS], F32, name="pick")
        nc.vector.tensor_reduce(pick[:], identity[:].rearrange("k (h g) -> k g h", h=HEADS), axis=AXIS.X, op=ALU.add)

        group = [P, ROWS, PATCHES]
        top = held.tile([P, ROWS], F32, name="top")
        nc.vector.reduce_max(top[:], raw[:], axis=AXIS.X)
        shift = held.tile([P, ROWS], F32, name="shift")
        nc.vector.tensor_scalar_mul(shift[:], top[:], -SCALE)
        e = held.tile(group, F32, name="e")
        norm = held.tile([P, ROWS], F32, name="norm")
        for i in range(ROWS):
            nc.scalar.activation(
                e[:, i, :], raw[:, i, :], FUNC.Exp, bias=shift[:, i : i + 1], scale=SCALE, accum_out=norm[:, i : i + 1]
            )
        inverse = held.tile([P, ROWS], F32, name="inverse")
        nc.vector.reciprocal(inverse[:], norm[:])
        share = held.tile(group, F32, name="share")
        nc.vector.scalar_tensor_tensor(
            share[:], e[:], 1.0 / HEADS, inverse[:].unsqueeze(2).to_broadcast(group), ALU.mult, ALU.mult
        )

        weights = held.tile([P, ENTRIES], F32, name="weights")
        for start, width in cuts(0, OPENING[0] + (BANK,) * ((ENTRIES - ROUND) // BANK)):
            bank = psum.tile([P, BANK], F32, name="bank")
            for q in range(width // RUN):
                g = start // RUN + q
                nc.tensor.matmul(
                    bank[:, q * RUN : (q + 1) * RUN],
                    pick[:, g : g + 1].to_broadcast([P, P]),
                    share[:].rearrange("k i t -> k (i t)"),
                    start=True,
                    stop=True,
                )
            nc.scalar.copy(weights[:, start : start + width], bank[:, :width])

        sums = held.tile([P, BLOCKS, PATCHES], F32, name="sums")
        total = totals.tile([P, BLOCKS, ROUND_PATCHES], F32, name="total")

        for m in range(ROUNDS):
            products = work.tile([P, BLOCKS, ROUND], F32, name="products")
            for b in range(BLOCKS):
                if m == ROUNDS - 1 and b == BLOCKS - 1:
                    nc.vector.tensor_copy(sums[:, :, 0:ROUND_PATCHES], total[:])
                if m == 0:
                    widths = OPENING[b]
                elif m < ROUNDS - 1:
                    widths = (ROUND,)
                else:
                    widths = (BANK,) * (ROUND // BANK)
                for at, width in cuts(0, widths):
                    start = m * ROUND + at
                    picked = tables[b][:].indirect(offsets[:, start // 16 : (start + width) // 16])
                    nc.vector.tensor_tensor(
                        products[:, b, at : at + width], picked, weights[:, start : start + width], ALU.mult
                    )
                    first = start // PATCHES
                    count = width // PATCHES
                    if m == 0:
                        pass
                    elif start + width == ENTRIES and b == BLOCKS - 1:
                        nc.vector.tensor_reduce(
                            sums[:, b, first : first + count],
                            products[:, b, at : at + width].rearrange("c (r t) -> c r t", t=PATCHES),
                            axis=AXIS.X,
                            op=ALU.add,
                        )
                    else:
                        for r in range(count):
                            unused = work.tile([P, PATCHES], BF16, name="unused")
                            nc.scalar.activation(
                                unused[:],
                                products[:, b, at + r * PATCHES : at + (r + 1) * PATCHES],
                                FUNC.Copy,
                                accum_out=sums[:, b, first + r : first + r + 1],
                            )
            if m == 0:
                by_key = products[:].rearrange("c b (r t) -> c (b r) t", t=PATCHES)
                for t in range(PATCHES):
                    nc.tensor.matmul(
                        total[:].rearrange("c b r -> c (b r)"),
                        identity[:],
                        by_key[:, :, t],
                        start=(t == 0),
                        stop=(t == PATCHES - 1),
                    )

        for b in range(BLOCKS):
            nc.sync.dma_start(out[b * P : (b + 1) * P, :], sums[:, b, :])
